import numpy as np
import ml_dtypes

BF16 = ml_dtypes.bfloat16


def bf(x):
    return np.asarray(x, np.float32).astype(BF16)


def f32(x):
    return np.asarray(x, np.float32)


def f64(x):
    return np.asarray(x).astype(np.float64)


def striped(idx):
    return np.tile(idx.reshape(-1, 16).T, (8, 1))


DIN, H, K, S, N = 128, 256, 3, 4096, 2048


def sigmoid(v):
    return 1.0 / (1.0 + np.exp(-v))


def setup_inputs():
    return {"base": f32(0.2 * np.random.standard_normal((H, S))), "x": bf(np.random.standard_normal((DIN, N))), "w": bf(np.random.standard_normal((DIN, K * H)) / np.sqrt(DIN)), "b": f32(0.1 * np.random.standard_normal((K * H, 1))), "offs": striped(np.random.permutation(S)[:N])}


def reference(base, x, w, b, offs):
    idx = offs[:16].T.reshape(-1)
    z = f64(w).T @ f64(x) + f64(b)
    zi, zo, zu = z.reshape(K, H, N)
    in_gate, out_gate, upd = sigmoid(zi), sigmoid(zo), np.tanh(zu)
    cell = in_gate * upd
    out = f64(base).copy()
    out[:, idx] = out_gate * np.tanh(cell)
    return out

@@ -1,0 +1,74 @@
+import concourse.mybir as mybir
+from concourse.masks import make_identity
+
+F32 = mybir.dt.float32
+BF16 = mybir.dt.bfloat16
+U16 = mybir.dt.uint16
+SIGMOID = mybir.ActivationFunctionType.Sigmoid
+TANH = mybir.ActivationFunctionType.Tanh
+MULT = mybir.AluOpType.mult
+
+P = 128
+DIN, H, GATES, S, N = 128, 256, 3, 4096, 2048
+BLOCKS = H // P
+BANK = 512
+IN_GATE, OUT_GATE, UPD = 0, 1, 2
+BIAS_ROWS = GATES * BLOCKS
+PAD_ROWS = 64
+
+FLOPS = 2 * DIN * GATES * H * N
+
+
+def tile_treelstm_kernel(tc, base, x, w, b, offs, out):
+    nc = tc.nc
+    with (
+        tc.tile_pool(name="held", bufs=1) as held,
+        tc.tile_pool(name="gates", bufs=2) as gates,
+        tc.psum_pool(name="once", bufs=1) as once,
+        tc.psum_pool(name="banks", bufs=6) as banks,
+    ):
+        w_sb = held.tile([DIN, GATES * H], BF16, name="w_sb")
+        nc.sync.dma_start(w_sb[:], w)
+        x_sb = held.tile([DIN, N], BF16, name="x_sb")
+        nc.sync.dma_start(x_sb[:], x)
+        b_rows = held.tile([PAD_ROWS, P], F32, name="b_rows")
+        nc.vector.memset(b_rows[:], 0.0)
+        nc.sync.dma_start(b_rows[0:BIAS_ROWS, :], b.rearrange("(k p) o -> k (p o)", p=P))
+        offsets = held.tile([P, N // 16], U16, name="offsets")
+        nc.sync.dma_start(offsets[:], offs)
+        windows = []
+        for h in range(BLOCKS):
+            window = held.tile([P, S], F32, name=f"window{h}")
+            nc.sync.dma_start(window[:], base[h * P : (h + 1) * P, :])
+            windows.append(window)
+
+        identity = held.tile([PAD_ROWS, PAD_ROWS], F32, name="identity")
+        make_identity(nc, identity[:])
+        bias_ps = once.tile([P, PAD_ROWS], F32, name="bias_ps")
+        nc.tensor.transpose(bias_ps[:], b_rows[:], identity[:])
+        bias = held.tile([P, BIAS_ROWS], F32, name="bias")
+        nc.vector.tensor_copy(bias[:], bias_ps[:, 0:BIAS_ROWS])
+
+        for h in range(BLOCKS):
+
+            def gate(g, func, name):
+                k = g * BLOCKS + h
+                values = gates.tile([P, N], F32, name=name)
+                for c in range(0, N, BANK):
+                    z = banks.tile([P, BANK], F32, name="z")
+                    nc.tensor.matmul(
+                        z[:], w_sb[:, k * P : (k + 1) * P], x_sb[:, c : c + BANK], start=True, stop=True
+                    )
+                    nc.scalar.activation(values[:, c : c + BANK], z[:], func, bias=bias[:, k : k + 1])
+                return values
+
+            in_gate = gate(IN_GATE, SIGMOID, "in_gate")
+            upd = gate(UPD, TANH, "upd")
+            cell = gates.tile([P, N], F32, name="cell")
+            nc.vector.tensor_tensor(cell[:], in_gate[:], upd[:], MULT)
+            out_gate = gate(OUT_GATE, SIGMOID, "out_gate")
+            tanh_cell = gates.tile([P, N], F32, name="tanh_cell")
+            nc.scalar.activation(tanh_cell[:], cell[:], TANH)
+
+            nc.vector.tensor_tensor(windows[h][:].indirect(offsets[:]), out_gate[:], tanh_cell[:], MULT)
+            nc.sync.dma_start(out[h * P : (h + 1) * P, :], windows[h][:])

@@ -12,6 +12,8 @@ P = 128
 DIN, H, GATES, S, N = 128, 256, 3, 4096, 2048
 BLOCKS = H // P
 BANK = 512
+PIECE = 1024
+PER_COLUMN = 16
 IN_GATE, OUT_GATE, UPD = 0, 1, 2
 BIAS_ROWS = GATES * BLOCKS
 PAD_ROWS = 64
@@ -23,9 +25,9 @@ def tile_treelstm_kernel(tc, base, x, w, b, offs, out):
     nc = tc.nc
     with (
         tc.tile_pool(name="held", bufs=1) as held,
-        tc.tile_pool(name="gates", bufs=2) as gates,
+        tc.tile_pool(name="gates", bufs=BLOCKS * (N // PIECE)) as gates,
         tc.psum_pool(name="once", bufs=1) as once,
-        tc.psum_pool(name="banks", bufs=6) as banks,
+        tc.psum_pool(name="banks", bufs=7) as banks,
     ):
         w_sb = held.tile([DIN, GATES * H], BF16, name="w_sb")
         nc.sync.dma_start(w_sb[:], w)
@@ -34,7 +36,7 @@ def tile_treelstm_kernel(tc, base, x, w, b, offs, out):
         b_rows = held.tile([PAD_ROWS, P], F32, name="b_rows")
         nc.vector.memset(b_rows[:], 0.0)
         nc.sync.dma_start(b_rows[0:BIAS_ROWS, :], b.rearrange("(k p) o -> k (p o)", p=P))
-        offsets = held.tile([P, N // 16], U16, name="offsets")
+        offsets = held.tile([P, N // PER_COLUMN], U16, name="offsets")
         nc.sync.dma_start(offsets[:], offs)
         windows = []
         for h in range(BLOCKS):
@@ -49,26 +51,31 @@ def tile_treelstm_kernel(tc, base, x, w, b, offs, out):
         bias = held.tile([P, BIAS_ROWS], F32, name="bias")
         nc.vector.tensor_copy(bias[:], bias_ps[:, 0:BIAS_ROWS])
 
+        def gate(g, h, first, func, name):
+            k = g * BLOCKS + h
+            values = gates.tile([P, PIECE], F32, name=name)
+            for c in range(0, PIECE, BANK):
+                z = banks.tile([P, BANK], F32, name="z")
+                nc.tensor.matmul(
+                    z[:],
+                    w_sb[:, k * P : (k + 1) * P],
+                    x_sb[:, first + c : first + c + BANK],
+                    start=True,
+                    stop=True,
+                )
+                nc.scalar.activation(values[:, c : c + BANK], z[:], func, bias=bias[:, k : k + 1])
+            return values
+
         for h in range(BLOCKS):
+            for first in range(0, N, PIECE):
+                in_gate = gate(IN_GATE, h, first, SIGMOID, "in_gate")
+                upd = gate(UPD, h, first, TANH, "upd")
+                cell = gates.tile([P, PIECE], F32, name="cell")
+                nc.vector.tensor_tensor(cell[:], in_gate[:], upd[:], MULT)
+                out_gate = gate(OUT_GATE, h, first, SIGMOID, "out_gate")
+                tanh_cell = gates.tile([P, PIECE], F32, name="tanh_cell")
+                nc.scalar.activation(tanh_cell[:], cell[:], TANH)
 
-            def gate(g, func, name):
-                k = g * BLOCKS + h
-                values = gates.tile([P, N], F32, name=name)
-                for c in range(0, N, BANK):
-                    z = banks.tile([P, BANK], F32, name="z")
-                    nc.tensor.matmul(
-                        z[:], w_sb[:, k * P : (k + 1) * P], x_sb[:, c : c + BANK], start=True, stop=True
-                    )
-                    nc.scalar.activation(values[:, c : c + BANK], z[:], func, bias=bias[:, k : k + 1])
-                return values
-
-            in_gate = gate(IN_GATE, SIGMOID, "in_gate")
-            upd = gate(UPD, TANH, "upd")
-            cell = gates.tile([P, N], F32, name="cell")
-            nc.vector.tensor_tensor(cell[:], in_gate[:], upd[:], MULT)
-            out_gate = gate(OUT_GATE, SIGMOID, "out_gate")
-            tanh_cell = gates.tile([P, N], F32, name="tanh_cell")
-            nc.scalar.activation(tanh_cell[:], cell[:], TANH)
-
-            nc.vector.tensor_tensor(windows[h][:].indirect(offsets[:]), out_gate[:], tanh_cell[:], MULT)
+                piece = offsets[:, first // PER_COLUMN : (first + PIECE) // PER_COLUMN]
+                nc.vector.tensor_tensor(windows[h][:].indirect(piece), out_gate[:], tanh_cell[:], MULT)
             nc.sync.dma_start(out[h * P : (h + 1) * P, :], windows[h][:])

@@ -29,13 +29,14 @@ def tile_treelstm_kernel(tc, base, x, w, b, offs, out):
         tc.psum_pool(name="once", bufs=1) as once,
         tc.psum_pool(name="banks", bufs=7) as banks,
     ):
+        b_rows = held.tile([PAD_ROWS, P], F32, name="b_rows")
+        nc.gpsimd.memset(b_rows[:], 0.0)
+        nc.scalar.dma_start(b_rows[0:BIAS_ROWS, :], b.rearrange("(k p) o -> k (p o)", p=P))
+
         w_sb = held.tile([DIN, GATES * H], BF16, name="w_sb")
         nc.sync.dma_start(w_sb[:], w)
         x_sb = held.tile([DIN, N], BF16, name="x_sb")
         nc.sync.dma_start(x_sb[:], x)
-        b_rows = held.tile([PAD_ROWS, P], F32, name="b_rows")
-        nc.vector.memset(b_rows[:], 0.0)
-        nc.sync.dma_start(b_rows[0:BIAS_ROWS, :], b.rearrange("(k p) o -> k (p o)", p=P))
         offsets = held.tile([P, N // PER_COLUMN], U16, name="offsets")
         nc.sync.dma_start(offsets[:], offs)
         windows = []
@@ -66,16 +67,30 @@ def tile_treelstm_kernel(tc, base, x, w, b, offs, out):
                 nc.scalar.activation(values[:, c : c + BANK], z[:], func, bias=bias[:, k : k + 1])
             return values
 
-        for h in range(BLOCKS):
-            for first in range(0, N, PIECE):
-                in_gate = gate(IN_GATE, h, first, SIGMOID, "in_gate")
-                upd = gate(UPD, h, first, TANH, "upd")
-                cell = gates.tile([P, PIECE], F32, name="cell")
-                nc.vector.tensor_tensor(cell[:], in_gate[:], upd[:], MULT)
-                out_gate = gate(OUT_GATE, h, first, SIGMOID, "out_gate")
-                tanh_cell = gates.tile([P, PIECE], F32, name="tanh_cell")
-                nc.scalar.activation(tanh_cell[:], cell[:], TANH)
+        def three_gates(h, first):
+            in_gate = gate(IN_GATE, h, first, SIGMOID, "in_gate")
+            upd = gate(UPD, h, first, TANH, "upd")
+            out_gate = gate(OUT_GATE, h, first, SIGMOID, "out_gate")
+            return in_gate, upd, out_gate
 
-                piece = offsets[:, first // PER_COLUMN : (first + PIECE) // PER_COLUMN]
-                nc.vector.tensor_tensor(windows[h][:].indirect(piece), out_gate[:], tanh_cell[:], MULT)
-            nc.sync.dma_start(out[h * P : (h + 1) * P, :], windows[h][:])
+        def tanh_of_cell(in_gate, upd):
+            cell = gates.tile([P, PIECE], F32, name="cell")
+            nc.vector.tensor_tensor(cell[:], in_gate[:], upd[:], MULT)
+            tanh_cell = gates.tile([P, PIECE], F32, name="tanh_cell")
+            nc.scalar.activation(tanh_cell[:], cell[:], TANH)
+            return tanh_cell
+
+        pieces = [(h, first) for h in range(BLOCKS) for first in range(0, N, PIECE)]
+        factors = []
+        for q, (h, first) in enumerate(pieces):
+            ahead = 0 if q == 0 else 1
+            fresh = pieces[len(factors) : q + ahead + 1]
+            fresh_gates = [three_gates(*piece) for piece in fresh]
+            for in_gate, upd, out_gate in fresh_gates:
+                factors.append((out_gate, tanh_of_cell(in_gate, upd)))
+
+            out_gate, tanh_cell = factors[q]
+            listed = offsets[:, first // PER_COLUMN : (first + PIECE) // PER_COLUMN]
+            nc.vector.tensor_tensor(windows[h][:].indirect(listed), out_gate[:], tanh_cell[:], MULT)
+            if first + PIECE == N:
+                nc.sync.dma_start(out[h * P : (h + 1) * P, :], windows[h][:])

@@ -1,5 +1,4 @@
 import concourse.mybir as mybir
-from concourse.masks import make_identity
 
 F32 = mybir.dt.float32
 BF16 = mybir.dt.bfloat16
@@ -16,7 +15,6 @@ PIECE = 1024
 PER_COLUMN = 16
 IN_GATE, OUT_GATE, UPD = 0, 1, 2
 BIAS_ROWS = GATES * BLOCKS
-PAD_ROWS = 64
 
 FLOPS = 2 * DIN * GATES * H * N
 
@@ -26,13 +24,11 @@ def tile_treelstm_kernel(tc, base, x, w, b, offs, out):
     with (
         tc.tile_pool(name="held", bufs=1) as held,
         tc.tile_pool(name="gates", bufs=BLOCKS * (N // PIECE)) as gates,
-        tc.psum_pool(name="once", bufs=1) as once,
-        tc.psum_pool(name="banks", bufs=7) as banks,
+        tc.psum_pool(name="banks", bufs=8) as banks,
     ):
-        b_rows = held.tile([PAD_ROWS, P], F32, name="b_rows")
-        nc.gpsimd.memset(b_rows[:], 0.0)
-        nc.scalar.dma_start(b_rows[0:BIAS_ROWS, :], b.rearrange("(k p) o -> k (p o)", p=P))
-
+        bias = held.tile([P, BIAS_ROWS], F32, name="bias")
+        with nc.allow_non_contiguous_dma(reason="768 single values, loaded once"):
+            nc.sync.dma_start(bias[:], b.rearrange("(k p) o -> p (k o)", p=P))
         w_sb = held.tile([DIN, GATES * H], BF16, name="w_sb")
         nc.sync.dma_start(w_sb[:], w)
         x_sb = held.tile([DIN, N], BF16, name="x_sb")
@@ -44,13 +40,6 @@ def tile_treelstm_kernel(tc, base, x, w, b, offs, out):
             window = held.tile([P, S], F32, name=f"window{h}")
             nc.sync.dma_start(window[:], base[h * P : (h + 1) * P, :])
             windows.append(window)
-
-        identity = held.tile([PAD_ROWS, PAD_ROWS], F32, name="identity")
-        make_identity(nc, identity[:])
-        bias_ps = once.tile([P, PAD_ROWS], F32, name="bias_ps")
-        nc.tensor.transpose(bias_ps[:], b_rows[:], identity[:])
-        bias = held.tile([P, BIAS_ROWS], F32, name="bias")
-        nc.vector.tensor_copy(bias[:], bias_ps[:, 0:BIAS_ROWS])
 
         def gate(g, h, first, func, name):
             k = g * BLOCKS + h
@@ -67,29 +56,22 @@ def tile_treelstm_kernel(tc, base, x, w, b, offs, out):
                 nc.scalar.activation(values[:, c : c + BANK], z[:], func, bias=bias[:, k : k + 1])
             return values
 
-        def three_gates(h, first):
+        def cell_of(h, first):
             in_gate = gate(IN_GATE, h, first, SIGMOID, "in_gate")
             upd = gate(UPD, h, first, TANH, "upd")
-            out_gate = gate(OUT_GATE, h, first, SIGMOID, "out_gate")
-            return in_gate, upd, out_gate
-
-        def tanh_of_cell(in_gate, upd):
             cell = gates.tile([P, PIECE], F32, name="cell")
             nc.vector.tensor_tensor(cell[:], in_gate[:], upd[:], MULT)
-            tanh_cell = gates.tile([P, PIECE], F32, name="tanh_cell")
-            nc.scalar.activation(tanh_cell[:], cell[:], TANH)
-            return tanh_cell
+            return cell
 
         pieces = [(h, first) for h in range(BLOCKS) for first in range(0, N, PIECE)]
-        factors = []
+        cells = [cell_of(*pieces[0])]
         for q, (h, first) in enumerate(pieces):
-            ahead = 0 if q == 0 else 1
-            fresh = pieces[len(factors) : q + ahead + 1]
-            fresh_gates = [three_gates(*piece) for piece in fresh]
-            for in_gate, upd, out_gate in fresh_gates:
-                factors.append((out_gate, tanh_of_cell(in_gate, upd)))
+            if q + 1 < len(pieces):
+                cells.append(cell_of(*pieces[q + 1]))
+            out_gate = gate(OUT_GATE, h, first, SIGMOID, "out_gate")
+            tanh_cell = gates.tile([P, PIECE], F32, name="tanh_cell")
+            nc.scalar.activation(tanh_cell[:], cells[q][:], TANH)
 
-            out_gate, tanh_cell = factors[q]
             listed = offsets[:, first // PER_COLUMN : (first + PIECE) // PER_COLUMN]
             nc.vector.tensor_tensor(windows[h][:].indirect(listed), out_gate[:], tanh_cell[:], MULT)
             if first + PIECE == N:

@@ -60,7 +60,7 @@ def tile_treelstm_kernel(tc, base, x, w, b, offs, out):
             in_gate = gate(IN_GATE, h, first, SIGMOID, "in_gate")
             upd = gate(UPD, h, first, TANH, "upd")
             cell = gates.tile([P, PIECE], F32, name="cell")
-            nc.vector.tensor_tensor(cell[:], in_gate[:], upd[:], MULT)
+            nc.gpsimd.tensor_tensor(cell[:], in_gate[:], upd[:], MULT)
             return cell
 
         pieces = [(h, first) for h in range(BLOCKS) for first in range(0, N, PIECE)]

@@ -26,13 +26,19 @@ def tile_treelstm_kernel(tc, base, x, w, b, offs, out):
         tc.tile_pool(name="gates", bufs=BLOCKS * (N // PIECE)) as gates,
         tc.psum_pool(name="banks", bufs=8) as banks,
     ):
+        scratch = held.tile([P, 1], F32, name="scratch")
+        nc.gpsimd.memset(scratch[:], 0.0)
+        nc.scalar.activation(scratch[:], scratch[:], SIGMOID)
+
         bias = held.tile([P, BIAS_ROWS], F32, name="bias")
         with nc.allow_non_contiguous_dma(reason="768 single values, loaded once"):
             nc.sync.dma_start(bias[:], b.rearrange("(k p) o -> p (k o)", p=P))
         w_sb = held.tile([DIN, GATES * H], BF16, name="w_sb")
         nc.sync.dma_start(w_sb[:], w)
-        x_sb = held.tile([DIN, N], BF16, name="x_sb")
-        nc.sync.dma_start(x_sb[:], x)
+        x_sb = {}
+        for first in range(0, N, PIECE):
+            x_sb[first] = held.tile([DIN, PIECE], BF16, name=f"x_sb{first}")
+            nc.sync.dma_start(x_sb[first][:], x[:, first : first + PIECE])
         offsets = held.tile([P, N // PER_COLUMN], U16, name="offsets")
         nc.sync.dma_start(offsets[:], offs)
         windows = []
@@ -49,7 +55,7 @@ def tile_treelstm_kernel(tc, base, x, w, b, offs, out):
                 nc.tensor.matmul(
                     z[:],
                     w_sb[:, k * P : (k + 1) * P],
-                    x_sb[:, first + c : first + c + BANK],
+                    x_sb[first][:, c : c + BANK],
                     start=True,
                     stop=True,
                 )
@@ -60,7 +66,7 @@ def tile_treelstm_kernel(tc, base, x, w, b, offs, out):
             in_gate = gate(IN_GATE, h, first, SIGMOID, "in_gate")
             upd = gate(UPD, h, first, TANH, "upd")
             cell = gates.tile([P, PIECE], F32, name="cell")
-            nc.gpsimd.tensor_tensor(cell[:], in_gate[:], upd[:], MULT)
+            nc.vector.tensor_tensor(cell[:], in_gate[:], upd[:], MULT)
             return cell
 
         pieces = [(h, first) for h in range(BLOCKS) for first in range(0, N, PIECE)]

@@ -1,4 +1,5 @@
 import concourse.mybir as mybir
+from concourse.masks import make_identity
 
 F32 = mybir.dt.float32
 BF16 = mybir.dt.bfloat16
@@ -15,6 +16,7 @@ PIECE = 1024
 PER_COLUMN = 16
 IN_GATE, OUT_GATE, UPD = 0, 1, 2
 BIAS_ROWS = GATES * BLOCKS
+PAD_ROWS = 64
 
 FLOPS = 2 * DIN * GATES * H * N
 
@@ -24,21 +26,16 @@ def tile_treelstm_kernel(tc, base, x, w, b, offs, out):
     with (
         tc.tile_pool(name="held", bufs=1) as held,
         tc.tile_pool(name="gates", bufs=BLOCKS * (N // PIECE)) as gates,
-        tc.psum_pool(name="banks", bufs=8) as banks,
+        tc.psum_pool(name="once", bufs=1) as once,
+        tc.psum_pool(name="banks", bufs=7) as banks,
     ):
-        scratch = held.tile([P, 1], F32, name="scratch")
-        nc.gpsimd.memset(scratch[:], 0.0)
-        nc.scalar.activation(scratch[:], scratch[:], SIGMOID)
-
-        bias = held.tile([P, BIAS_ROWS], F32, name="bias")
-        with nc.allow_non_contiguous_dma(reason="768 single values, loaded once"):
-            nc.sync.dma_start(bias[:], b.rearrange("(k p) o -> p (k o)", p=P))
+        b_rows = held.tile([PAD_ROWS, P], F32, name="b_rows")
+        nc.gpsimd.memset(b_rows[:], 0.0)
+        nc.sync.dma_start(b_rows[0:BIAS_ROWS, :], b.rearrange("(k p) o -> k (p o)", p=P))
         w_sb = held.tile([DIN, GATES * H], BF16, name="w_sb")
         nc.sync.dma_start(w_sb[:], w)
-        x_sb = {}
-        for first in range(0, N, PIECE):
-            x_sb[first] = held.tile([DIN, PIECE], BF16, name=f"x_sb{first}")
-            nc.sync.dma_start(x_sb[first][:], x[:, first : first + PIECE])
+        x_sb = held.tile([DIN, N], BF16, name="x_sb")
+        nc.sync.dma_start(x_sb[:], x)
         offsets = held.tile([P, N // PER_COLUMN], U16, name="offsets")
         nc.sync.dma_start(offsets[:], offs)
         windows = []
@@ -46,6 +43,13 @@ def tile_treelstm_kernel(tc, base, x, w, b, offs, out):
             window = held.tile([P, S], F32, name=f"window{h}")
             nc.sync.dma_start(window[:], base[h * P : (h + 1) * P, :])
             windows.append(window)
+
+        identity = held.tile([PAD_ROWS, PAD_ROWS], F32, name="identity")
+        make_identity(nc, identity[:])
+        bias_ps = once.tile([P, PAD_ROWS], F32, name="bias_ps")
+        nc.tensor.transpose(bias_ps[:], b_rows[:], identity[:])
+        bias = held.tile([P, BIAS_ROWS], F32, name="bias")
+        nc.vector.tensor_copy(bias[:], bias_ps[:, 0:BIAS_ROWS])
 
         def gate(g, h, first, func, name):
             k = g * BLOCKS + h
@@ -55,7 +59,7 @@ def tile_treelstm_kernel(tc, base, x, w, b, offs, out):
                 nc.tensor.matmul(
                     z[:],
                     w_sb[:, k * P : (k + 1) * P],
-                    x_sb[first][:, c : c + BANK],
+                    x_sb[:, first + c : first + c + BANK],
                     start=True,
                     stop=True,
                 )

@@ -1,5 +1,4 @@
 import concourse.mybir as mybir
-from concourse.masks import make_identity
 
 F32 = mybir.dt.float32
 BF16 = mybir.dt.bfloat16
@@ -16,7 +15,6 @@ PIECE = 1024
 PER_COLUMN = 16
 IN_GATE, OUT_GATE, UPD = 0, 1, 2
 BIAS_ROWS = GATES * BLOCKS
-PAD_ROWS = 64
 
 FLOPS = 2 * DIN * GATES * H * N
 
@@ -26,16 +24,21 @@ def tile_treelstm_kernel(tc, base, x, w, b, offs, out):
     with (
         tc.tile_pool(name="held", bufs=1) as held,
         tc.tile_pool(name="gates", bufs=BLOCKS * (N // PIECE)) as gates,
-        tc.psum_pool(name="once", bufs=1) as once,
-        tc.psum_pool(name="banks", bufs=7) as banks,
+        tc.psum_pool(name="banks", bufs=8) as banks,
     ):
-        b_rows = held.tile([PAD_ROWS, P], F32, name="b_rows")
-        nc.gpsimd.memset(b_rows[:], 0.0)
-        nc.sync.dma_start(b_rows[0:BIAS_ROWS, :], b.rearrange("(k p) o -> k (p o)", p=P))
+        scratch = held.tile([P, 1], F32, name="scratch")
+        nc.gpsimd.memset(scratch[:], 0.0)
+        nc.scalar.activation(scratch[:], scratch[:], SIGMOID)
+
         w_sb = held.tile([DIN, GATES * H], BF16, name="w_sb")
         nc.sync.dma_start(w_sb[:], w)
-        x_sb = held.tile([DIN, N], BF16, name="x_sb")
-        nc.sync.dma_start(x_sb[:], x)
+        x_sb = {first: held.tile([DIN, PIECE], BF16, name=f"x_sb{first}") for first in range(0, N, PIECE)}
+        nc.sync.dma_start(x_sb[0][:], x[:, 0:PIECE])
+        bias = held.tile([P, BIAS_ROWS], F32, name="bias")
+        with nc.allow_non_contiguous_dma(reason="768 single values, loaded once"):
+            nc.sync.dma_start(bias[:], b.rearrange("(k p) o -> p (k o)", p=P))
+        for first in range(PIECE, N, PIECE):
+            nc.sync.dma_start(x_sb[first][:], x[:, first : first + PIECE])
         offsets = held.tile([P, N // PER_COLUMN], U16, name="offsets")
         nc.sync.dma_start(offsets[:], offs)
         windows = []
@@ -43,13 +46,6 @@ def tile_treelstm_kernel(tc, base, x, w, b, offs, out):
             window = held.tile([P, S], F32, name=f"window{h}")
             nc.sync.dma_start(window[:], base[h * P : (h + 1) * P, :])
             windows.append(window)
-
-        identity = held.tile([PAD_ROWS, PAD_ROWS], F32, name="identity")
-        make_identity(nc, identity[:])
-        bias_ps = once.tile([P, PAD_ROWS], F32, name="bias_ps")
-        nc.tensor.transpose(bias_ps[:], b_rows[:], identity[:])
-        bias = held.tile([P, BIAS_ROWS], F32, name="bias")
-        nc.vector.tensor_copy(bias[:], bias_ps[:, 0:BIAS_ROWS])
 
         def gate(g, h, first, func, name):
             k = g * BLOCKS + h
@@ -59,7 +55,7 @@ def tile_treelstm_kernel(tc, base, x, w, b, offs, out):
                 nc.tensor.matmul(
                     z[:],
                     w_sb[:, k * P : (k + 1) * P],
-                    x_sb[:, first + c : first + c + BANK],
+                    x_sb[first][:, c : c + BANK],
                     start=True,
                     stop=True,
                 )

@@ -11,7 +11,8 @@ P = 128
 DIN, H, GATES, S, N = 128, 256, 3, 4096, 2048
 BLOCKS = H // P
 BANK = 512
-PIECE = 1024
+PIECE = BANK
+X_LOAD = 1024
 PER_COLUMN = 16
 IN_GATE, OUT_GATE, UPD = 0, 1, 2
 BIAS_ROWS = GATES * BLOCKS
@@ -32,34 +33,33 @@ def tile_treelstm_kernel(tc, base, x, w, b, offs, out):
 
         w_sb = held.tile([DIN, GATES * H], BF16, name="w_sb")
         nc.sync.dma_start(w_sb[:], w)
-        x_sb = {first: held.tile([DIN, PIECE], BF16, name=f"x_sb{first}") for first in range(0, N, PIECE)}
-        nc.sync.dma_start(x_sb[0][:], x[:, 0:PIECE])
+        x_sb = {start: held.tile([DIN, X_LOAD], BF16, name=f"x_sb{start}") for start in range(0, N, X_LOAD)}
+        nc.sync.dma_start(x_sb[0][:], x[:, 0:X_LOAD])
         bias = held.tile([P, BIAS_ROWS], F32, name="bias")
         with nc.allow_non_contiguous_dma(reason="768 single values, loaded once"):
             nc.sync.dma_start(bias[:], b.rearrange("(k p) o -> p (k o)", p=P))
-        for first in range(PIECE, N, PIECE):
-            nc.sync.dma_start(x_sb[first][:], x[:, first : first + PIECE])
         offsets = held.tile([P, N // PER_COLUMN], U16, name="offsets")
         nc.sync.dma_start(offsets[:], offs)
-        windows = []
-        for h in range(BLOCKS):
-            window = held.tile([P, S], F32, name=f"window{h}")
-            nc.sync.dma_start(window[:], base[h * P : (h + 1) * P, :])
-            windows.append(window)
+        windows = [held.tile([P, S], F32, name=f"window{h}") for h in range(BLOCKS)]
+        nc.sync.dma_start(windows[0][:], base[0:P, :])
+        for start in range(X_LOAD, N, X_LOAD):
+            nc.sync.dma_start(x_sb[start][:], x[:, start : start + X_LOAD])
+        for h in range(1, BLOCKS):
+            nc.sync.dma_start(windows[h][:], base[h * P : (h + 1) * P, :])
 
         def gate(g, h, first, func, name):
             k = g * BLOCKS + h
+            start = first - first % X_LOAD
+            z = banks.tile([P, PIECE], F32, name="z")
+            nc.tensor.matmul(
+                z[:],
+                w_sb[:, k * P : (k + 1) * P],
+                x_sb[start][:, first - start : first - start + PIECE],
+                start=True,
+                stop=True,
+            )
             values = gates.tile([P, PIECE], F32, name=name)
-            for c in range(0, PIECE, BANK):
-                z = banks.tile([P, BANK], F32, name="z")
-                nc.tensor.matmul(
-                    z[:],
-                    w_sb[:, k * P : (k + 1) * P],
-                    x_sb[first][:, c : c + BANK],
-                    start=True,
-                    stop=True,
-                )
-                nc.scalar.activation(values[:, c : c + BANK], z[:], func, bias=bias[:, k : k + 1])
+            nc.scalar.activation(values[:], z[:], func, bias=bias[:, k : k + 1])
             return values
 
         def cell_of(h, first):

@@ -27,6 +27,9 @@ def tile_treelstm_kernel(tc, base, x, w, b, offs, out):
         tc.tile_pool(name="gates", bufs=BLOCKS * (N // PIECE)) as gates,
         tc.psum_pool(name="banks", bufs=8) as banks,
     ):
+        bias = held.tile([P, BIAS_ROWS], F32, name="bias")
+        with nc.allow_non_contiguous_dma(reason="768 single values, loaded once"):
+            nc.scalar.dma_start(bias[:], b.rearrange("(k p) o -> p (k o)", p=P))
         scratch = held.tile([P, 1], F32, name="scratch")
         nc.gpsimd.memset(scratch[:], 0.0)
         nc.scalar.activation(scratch[:], scratch[:], SIGMOID)
@@ -35,9 +38,6 @@ def tile_treelstm_kernel(tc, base, x, w, b, offs, out):
         nc.sync.dma_start(w_sb[:], w)
         x_sb = {start: held.tile([DIN, X_LOAD], BF16, name=f"x_sb{start}") for start in range(0, N, X_LOAD)}
         nc.sync.dma_start(x_sb[0][:], x[:, 0:X_LOAD])
-        bias = held.tile([P, BIAS_ROWS], F32, name="bias")
-        with nc.allow_non_contiguous_dma(reason="768 single values, loaded once"):
-            nc.sync.dma_start(bias[:], b.rearrange("(k p) o -> p (k o)", p=P))
         offsets = held.tile([P, N // PER_COLUMN], U16, name="offsets")
         nc.sync.dma_start(offsets[:], offs)
         windows = [held.tile([P, S], F32, name=f"window{h}") for h in range(BLOCKS)]

@@ -28,8 +28,13 @@ def tile_treelstm_kernel(tc, base, x, w, b, offs, out):
         tc.psum_pool(name="banks", bufs=8) as banks,
     ):
         bias = held.tile([P, BIAS_ROWS], F32, name="bias")
-        with nc.allow_non_contiguous_dma(reason="768 single values, loaded once"):
-            nc.scalar.dma_start(bias[:], b.rearrange("(k p) o -> p (k o)", p=P))
+        with nc.allow_non_contiguous_dma(reason="384 runs of two values, loaded once"):
+            nc.scalar.dma_start(
+                bias[:].rearrange("p (g h) -> p g h", g=GATES),
+                b.rearrange("(g p h) o -> p g (h o)", g=GATES, h=BLOCKS),
+            )
+        base_blocks = base.rearrange("(p h) s -> h p s", h=BLOCKS)
+        out_blocks = out.rearrange("(p h) s -> h p s", h=BLOCKS)
         scratch = held.tile([P, 1], F32, name="scratch")
         nc.gpsimd.memset(scratch[:], 0.0)
         nc.scalar.activation(scratch[:], scratch[:], SIGMOID)
@@ -41,11 +46,11 @@ def tile_treelstm_kernel(tc, base, x, w, b, offs, out):
         offsets = held.tile([P, N // PER_COLUMN], U16, name="offsets")
         nc.sync.dma_start(offsets[:], offs)
         windows = [held.tile([P, S], F32, name=f"window{h}") for h in range(BLOCKS)]
-        nc.sync.dma_start(windows[0][:], base[0:P, :])
+        nc.sync.dma_start(windows[0][:], base_blocks[0])
         for start in range(X_LOAD, N, X_LOAD):
             nc.sync.dma_start(x_sb[start][:], x[:, start : start + X_LOAD])
         for h in range(1, BLOCKS):
-            nc.sync.dma_start(windows[h][:], base[h * P : (h + 1) * P, :])
+            nc.sync.dma_start(windows[h][:], base_blocks[h])
 
         def gate(g, h, first, func, name):
             k = g * BLOCKS + h
@@ -53,7 +58,7 @@ def tile_treelstm_kernel(tc, base, x, w, b, offs, out):
             z = banks.tile([P, PIECE], F32, name="z")
             nc.tensor.matmul(
                 z[:],
-                w_sb[:, k * P : (k + 1) * P],
+                w_sb[:, g * H + h : (g + 1) * H : BLOCKS],
                 x_sb[start][:, first - start : first - start + PIECE],
                 start=True,
                 stop=True,
@@ -81,4 +86,4 @@ def tile_treelstm_kernel(tc, base, x, w, b, offs, out):
             listed = offsets[:, first // PER_COLUMN : (first + PIECE) // PER_COLUMN]
             nc.vector.tensor_tensor(windows[h][:].indirect(listed), out_gate[:], tanh_cell[:], MULT)
             if first + PIECE == N:
-                nc.sync.dma_start(out[h * P : (h + 1) * P, :], windows[h][:])
+                nc.sync.dma_start(out_blocks[h], windows[h][:])

@@ -24,7 +24,7 @@ def tile_treelstm_kernel(tc, base, x, w, b, offs, out):
     nc = tc.nc
     with (
         tc.tile_pool(name="held", bufs=1) as held,
-        tc.tile_pool(name="gates", bufs=BLOCKS * (N // PIECE)) as gates,
+        tc.tile_pool(name="gates", bufs=BLOCKS * (N // PIECE) - 1) as gates,
         tc.psum_pool(name="banks", bufs=8) as banks,
     ):
         bias = held.tile([P, BIAS_ROWS], F32, name="bias")
@@ -52,38 +52,47 @@ def tile_treelstm_kernel(tc, base, x, w, b, offs, out):
         for h in range(1, BLOCKS):
             nc.sync.dma_start(windows[h][:], base_blocks[h])
 
-        def gate(g, h, first, func, name):
+        def gate(g, h, first, width, func, name):
             k = g * BLOCKS + h
-            start = first - first % X_LOAD
-            z = banks.tile([P, PIECE], F32, name="z")
-            nc.tensor.matmul(
-                z[:],
-                w_sb[:, g * H + h : (g + 1) * H : BLOCKS],
-                x_sb[start][:, first - start : first - start + PIECE],
-                start=True,
-                stop=True,
-            )
-            values = gates.tile([P, PIECE], F32, name=name)
-            nc.scalar.activation(values[:], z[:], func, bias=bias[:, k : k + 1])
+            values = gates.tile([P, width], F32, name=name)
+            for at in range(first, first + width, BANK):
+                start = at - at % X_LOAD
+                z = banks.tile([P, BANK], F32, name="z")
+                nc.tensor.matmul(
+                    z[:],
+                    w_sb[:, g * H + h : (g + 1) * H : BLOCKS],
+                    x_sb[start][:, at - start : at - start + BANK],
+                    start=True,
+                    stop=True,
+                )
+                nc.scalar.activation(values[:, at - first : at - first + BANK], z[:], func, bias=bias[:, k : k + 1])
             return values
 
-        def cell_of(h, first):
-            in_gate = gate(IN_GATE, h, first, SIGMOID, "in_gate")
-            upd = gate(UPD, h, first, TANH, "upd")
-            cell = gates.tile([P, PIECE], F32, name="cell")
+        def cell_of(h, first, width):
+            in_gate = gate(IN_GATE, h, first, width, SIGMOID, "in_gate")
+            upd = gate(UPD, h, first, width, TANH, "upd")
+            cell = gates.tile([P, width], F32, name="cell")
             nc.vector.tensor_tensor(cell[:], in_gate[:], upd[:], MULT)
             return cell
 
-        pieces = [(h, first) for h in range(BLOCKS) for first in range(0, N, PIECE)]
+        pieces = [
+            (0, 0, PIECE),
+            (0, PIECE, PIECE),
+            (0, 2 * PIECE, PIECE),
+            (1, 0, PIECE),
+            (1, PIECE, PIECE),
+            (0, 3 * PIECE, PIECE),
+            (1, 2 * PIECE, 2 * PIECE),
+        ]
         cells = [cell_of(*pieces[0])]
-        for q, (h, first) in enumerate(pieces):
+        for q, (h, first, width) in enumerate(pieces):
             if q + 1 < len(pieces):
                 cells.append(cell_of(*pieces[q + 1]))
-            out_gate = gate(OUT_GATE, h, first, SIGMOID, "out_gate")
-            tanh_cell = gates.tile([P, PIECE], F32, name="tanh_cell")
+            out_gate = gate(OUT_GATE, h, first, width, SIGMOID, "out_gate")
+            tanh_cell = gates.tile([P, width], F32, name="tanh_cell")
             nc.scalar.activation(tanh_cell[:], cells[q][:], TANH)
 
-            listed = offsets[:, first // PER_COLUMN : (first + PIECE) // PER_COLUMN]
+            listed = offsets[:, first // PER_COLUMN : (first + width) // PER_COLUMN]
             nc.vector.tensor_tensor(windows[h][:].indirect(listed), out_gate[:], tanh_cell[:], MULT)
-            if first + PIECE == N:
+            if first + width == N:
                 nc.sync.dma_start(out_blocks[h], windows[h][:])

@@ -1,10 +1,12 @@
 import concourse.mybir as mybir
+from concourse.masks import make_identity
 
 F32 = mybir.dt.float32
 BF16 = mybir.dt.bfloat16
 U16 = mybir.dt.uint16
 SIGMOID = mybir.ActivationFunctionType.Sigmoid
 TANH = mybir.ActivationFunctionType.Tanh
+SQUARE = mybir.ActivationFunctionType.Square
 MULT = mybir.AluOpType.mult
 
 P = 128
@@ -39,6 +41,11 @@ def tile_treelstm_kernel(tc, base, x, w, b, offs, out):
         nc.gpsimd.memset(scratch[:], 0.0)
         nc.scalar.activation(scratch[:], scratch[:], SIGMOID)
 
+        plus = held.tile([P, P], F32, name="plus")
+        make_identity(nc, plus[:])
+        minus = held.tile([P, P], F32, name="minus")
+        nc.gpsimd.tensor_scalar(minus[:], plus[:], -1.0, None, MULT)
+
         w_sb = held.tile([DIN, GATES * H], BF16, name="w_sb")
         nc.sync.dma_start(w_sb[:], w)
         x_sb = {start: held.tile([DIN, X_LOAD], BF16, name=f"x_sb{start}") for start in range(0, N, X_LOAD)}
@@ -52,47 +59,84 @@ def tile_treelstm_kernel(tc, base, x, w, b, offs, out):
         for h in range(1, BLOCKS):
             nc.sync.dma_start(windows[h][:], base_blocks[h])
 
-        def gate(g, h, first, width, func, name):
+        def gate(g, h, first, values, func):
             k = g * BLOCKS + h
-            values = gates.tile([P, width], F32, name=name)
-            for at in range(first, first + width, BANK):
-                start = at - at % X_LOAD
-                z = banks.tile([P, BANK], F32, name="z")
-                nc.tensor.matmul(
-                    z[:],
-                    w_sb[:, g * H + h : (g + 1) * H : BLOCKS],
-                    x_sb[start][:, at - start : at - start + BANK],
-                    start=True,
-                    stop=True,
-                )
-                nc.scalar.activation(values[:, at - first : at - first + BANK], z[:], func, bias=bias[:, k : k + 1])
-            return values
+            start = first - first % X_LOAD
+            z = banks.tile([P, PIECE], F32, name="z")
+            nc.tensor.matmul(
+                z[:],
+                w_sb[:, g * H + h : (g + 1) * H : BLOCKS],
+                x_sb[start][:, first - start : first - start + PIECE],
+                start=True,
+                stop=True,
+            )
+            nc.scalar.activation(values, z[:], func, bias=bias[:, k : k + 1])
 
-        def cell_of(h, first, width):
-            in_gate = gate(IN_GATE, h, first, width, SIGMOID, "in_gate")
-            upd = gate(UPD, h, first, width, TANH, "upd")
-            cell = gates.tile([P, width], F32, name="cell")
+        def factors_of(h, first):
+            in_gate = gates.tile([P, PIECE], F32, name="in_gate")
+            gate(IN_GATE, h, first, in_gate[:], SIGMOID)
+            upd = gates.tile([P, PIECE], F32, name="upd")
+            gate(UPD, h, first, upd[:], TANH)
+            return in_gate, upd
+
+        def product_of(in_gate, upd):
+            cell = gates.tile([P, PIECE], F32, name="cell")
             nc.vector.tensor_tensor(cell[:], in_gate[:], upd[:], MULT)
             return cell
 
-        pieces = [
-            (0, 0, PIECE),
-            (0, PIECE, PIECE),
-            (0, 2 * PIECE, PIECE),
-            (1, 0, PIECE),
-            (1, PIECE, PIECE),
-            (0, 3 * PIECE, PIECE),
-            (1, 2 * PIECE, 2 * PIECE),
+        def sum_of(left, sign, right):
+            z = banks.tile([P, PIECE], F32, name="z")
+            nc.tensor.matmul(z[:], plus[:], left[:], start=True, stop=False)
+            nc.tensor.matmul(z[:], sign[:], right[:], start=False, stop=True)
+            return z
+
+        def square_of_half(z, name):
+            square = gates.tile([P, PIECE], F32, name=name)
+            nc.scalar.activation(square[:], z[:], SQUARE, scale=0.5)
+            return square
+
+        scatters = [
+            [(0, 0)],
+            [(0, PIECE)],
+            [(0, 2 * PIECE)],
+            [(1, 3 * PIECE)],
+            [(1, 0)],
+            [(0, 3 * PIECE)],
+            [(1, PIECE), (1, 2 * PIECE)],
         ]
-        cells = [cell_of(*pieces[0])]
-        for q, (h, first, width) in enumerate(pieces):
-            if q + 1 < len(pieces):
-                cells.append(cell_of(*pieces[q + 1]))
-            out_gate = gate(OUT_GATE, h, first, width, SIGMOID, "out_gate")
+        by_vector = [(0, 0), (0, PIECE), (0, 2 * PIECE), (1, 3 * PIECE), (1, 2 * PIECE), (0, 3 * PIECE)]
+        by_squares = {0: (1, 0), 3: (1, PIECE)}
+        factors, half_sum, half_diff, cells = {}, {}, {}, {}
+
+        def squares_stage(stage, unit):
+            if stage == 1:
+                half_sum[unit] = sum_of(factors[unit][0], plus, factors[unit][1])
+            elif stage == 2:
+                half_sum[unit] = square_of_half(half_sum[unit], "half_sum")
+                half_diff[unit] = sum_of(factors[unit][0], minus, factors[unit][1])
+            elif stage == 3:
+                half_diff[unit] = square_of_half(half_diff[unit], "half_diff")
+                cells[unit] = sum_of(half_sum[unit], minus, half_diff[unit])
+
+        cells[by_vector[0]] = product_of(*factors_of(*by_vector[0]))
+        for q, units in enumerate(scatters):
+            if q + 1 < len(by_vector):
+                cells[by_vector[q + 1]] = product_of(*factors_of(*by_vector[q + 1]))
+            h, first = units[0]
+            width = len(units) * PIECE
+            parts = [slice(at, at + PIECE) for at in range(0, width, PIECE)]
+            out_gate = gates.tile([P, width], F32, name="out_gate")
+            for unit, part in zip(units, parts):
+                gate(OUT_GATE, *unit, out_gate[:, part], SIGMOID)
+            for begin, unit in by_squares.items():
+                squares_stage(q - begin, unit)
             tanh_cell = gates.tile([P, width], F32, name="tanh_cell")
-            nc.scalar.activation(tanh_cell[:], cells[q][:], TANH)
+            for unit, part in zip(units, parts):
+                nc.scalar.activation(tanh_cell[:, part], cells[unit][:], TANH)
 
             listed = offsets[:, first // PER_COLUMN : (first + width) // PER_COLUMN]
             nc.vector.tensor_tensor(windows[h][:].indirect(listed), out_gate[:], tanh_cell[:], MULT)
-            if first + width == N:
+            if all(later[0][0] != h for later in scatters[q + 1 :]):
                 nc.sync.dma_start(out_blocks[h], windows[h][:])
+            if q in by_squares:
+                factors[by_squares[q]] = factors_of(*by_squares[q])

@@ -10,6 +10,8 @@ SQUARE = mybir.ActivationFunctionType.Square
 MULT = mybir.AluOpType.mult
 
 P = 128
+HALF = P // 2
+LOW, HIGH = slice(0, HALF), slice(HALF, P)
 DIN, H, GATES, S, N = 128, 256, 3, 4096, 2048
 BLOCKS = H // P
 BANK = 512
@@ -41,10 +43,17 @@ def tile_treelstm_kernel(tc, base, x, w, b, offs, out):
         nc.gpsimd.memset(scratch[:], 0.0)
         nc.scalar.activation(scratch[:], scratch[:], SIGMOID)
 
-        plus = held.tile([P, P], F32, name="plus")
-        make_identity(nc, plus[:])
-        minus = held.tile([P, P], F32, name="minus")
-        nc.gpsimd.tensor_scalar(minus[:], plus[:], -1.0, None, MULT)
+        one = held.tile([P, P], F32, name="one")
+        make_identity(nc, one[:])
+        mix = held.tile([P, P], F32, name="mix")
+        nc.gpsimd.tensor_scalar(mix[LOW, LOW], one[LOW, LOW], 0.5, None, MULT)
+        nc.gpsimd.tensor_scalar(mix[LOW, HIGH], one[LOW, LOW], 0.5, None, MULT)
+        nc.gpsimd.tensor_copy(mix[HIGH, LOW], one[HIGH, HIGH])
+        nc.gpsimd.tensor_scalar(mix[HIGH, HIGH], one[HIGH, HIGH], -1.0, None, MULT)
+        spread = held.tile([P, 3 * HALF], F32, name="spread")
+        nc.gpsimd.memset(spread[:], 0.0)
+        nc.gpsimd.tensor_copy(spread[LOW, HIGH], one[LOW, LOW])
+        nc.gpsimd.tensor_scalar(spread[HIGH, HIGH], one[HIGH, HIGH], -1.0, None, MULT)
 
         w_sb = held.tile([DIN, GATES * H], BF16, name="w_sb")
         nc.sync.dma_start(w_sb[:], w)
@@ -54,8 +63,19 @@ def tile_treelstm_kernel(tc, base, x, w, b, offs, out):
         nc.sync.dma_start(offsets[:], offs)
         windows = [held.tile([P, S], F32, name=f"window{h}") for h in range(BLOCKS)]
         nc.sync.dma_start(windows[0][:], base_blocks[0])
+        bias_pair = held.tile([P, 2], F32, name="bias_pair")
+        b_pair = b.rearrange("(g k c h) o -> g h c (k o)", g=GATES, k=2, h=BLOCKS)
+        with nc.allow_non_contiguous_dma(reason="256 single values, loaded once"):
+            nc.sync.dma_start(bias_pair[LOW, :], b_pair[IN_GATE, 1])
+            nc.sync.dma_start(bias_pair[HIGH, :], b_pair[UPD, 1])
         for start in range(X_LOAD, N, X_LOAD):
             nc.sync.dma_start(x_sb[start][:], x[:, start : start + X_LOAD])
+        nc.scalar.mul(bias_pair[LOW, :], bias_pair[LOW, :], 0.5)
+        w_pair = held.tile([DIN, 2 * P], BF16, name="w_pair")
+        w_pair_parts = w_pair[:].rearrange("d (k s c) -> s d k c", k=2, s=2)
+        for part, g, factor in ((0, IN_GATE, 0.5), (1, UPD, 1.0)):
+            columns = w_sb[:, g * H + 1 : (g + 1) * H : BLOCKS].rearrange("d (k c) -> d k c", k=2)
+            nc.vector.tensor_scalar(w_pair_parts[part], columns, factor, None, MULT)
         for h in range(1, BLOCKS):
             nc.sync.dma_start(windows[h][:], base_blocks[h])
 
@@ -84,39 +104,49 @@ def tile_treelstm_kernel(tc, base, x, w, b, offs, out):
             nc.vector.tensor_tensor(cell[:], in_gate[:], upd[:], MULT)
             return cell
 
-        def sum_of(left, sign, right):
+        def pairs_of(first):
+            pairs = []
+            for k in range(2):
+                z = banks.tile([P, PIECE], F32, name="z")
+                start = first - first % X_LOAD
+                nc.tensor.matmul(
+                    z[:],
+                    w_pair[:, k * P : (k + 1) * P],
+                    x_sb[start][:, first - start : first - start + PIECE],
+                    start=True,
+                    stop=True,
+                )
+                pair = gates.tile([P, PIECE], F32, name=f"pair{k}")
+                nc.scalar.activation(pair[:], z[:], TANH, bias=bias_pair[:, k : k + 1])
+                pairs.append(pair)
+            return pairs
+
+        def mixed(pair):
             z = banks.tile([P, PIECE], F32, name="z")
-            nc.tensor.matmul(z[:], plus[:], left[:], start=True, stop=False)
-            nc.tensor.matmul(z[:], sign[:], right[:], start=False, stop=True)
+            nc.tensor.matmul(z[:], mix[:], pair[:], start=True, stop=True)
             return z
 
-        def square_of_half(z, name):
-            square = gates.tile([P, PIECE], F32, name=name)
-            nc.scalar.activation(square[:], z[:], SQUARE, scale=0.5)
-            return square
+        def product_by_squares(sums):
+            cell = banks.tile([P, PIECE], F32, name="z")
+            for k, z in enumerate(sums):
+                square = gates.tile([P, PIECE], F32, name=f"square{k}")
+                nc.scalar.activation(square[:], z[:], SQUARE, bias=0.25, scale=0.5)
+                place = spread[:, (1 - k) * HALF : (1 - k) * HALF + P]
+                nc.tensor.matmul(cell[:], place, square[:], start=k == 0, stop=k == 1)
+            return cell
 
         scatters = [
             [(0, 0)],
             [(0, PIECE)],
-            [(0, 2 * PIECE)],
             [(1, 3 * PIECE)],
+            [(0, 2 * PIECE)],
             [(1, 0)],
             [(0, 3 * PIECE)],
             [(1, PIECE), (1, 2 * PIECE)],
         ]
-        by_vector = [(0, 0), (0, PIECE), (0, 2 * PIECE), (1, 3 * PIECE), (1, 2 * PIECE), (0, 3 * PIECE)]
-        by_squares = {0: (1, 0), 3: (1, PIECE)}
-        factors, half_sum, half_diff, cells = {}, {}, {}, {}
-
-        def squares_stage(stage, unit):
-            if stage == 1:
-                half_sum[unit] = sum_of(factors[unit][0], plus, factors[unit][1])
-            elif stage == 2:
-                half_sum[unit] = square_of_half(half_sum[unit], "half_sum")
-                half_diff[unit] = sum_of(factors[unit][0], minus, factors[unit][1])
-            elif stage == 3:
-                half_diff[unit] = square_of_half(half_diff[unit], "half_diff")
-                cells[unit] = sum_of(half_sum[unit], minus, half_diff[unit])
+        by_vector = [(0, 0), (0, PIECE), (1, 3 * PIECE), (0, 2 * PIECE), (0, 3 * PIECE)]
+        by_squares = {0: (1, 0), 2: (1, PIECE), 4: (1, 2 * PIECE)}
+        factors, sums, cells = {}, {}, {}
 
         cells[by_vector[0]] = product_of(*factors_of(*by_vector[0]))
         for q, units in enumerate(scatters):
@@ -129,7 +159,10 @@ def tile_treelstm_kernel(tc, base, x, w, b, offs, out):
             for unit, part in zip(units, parts):
                 gate(OUT_GATE, *unit, out_gate[:, part], SIGMOID)
             for begin, unit in by_squares.items():
-                squares_stage(q - begin, unit)
+                if q == begin + 1:
+                    sums[unit] = [mixed(pair) for pair in factors[unit]]
+                elif q == begin + 2:
+                    cells[unit] = product_by_squares(sums[unit])
             tanh_cell = gates.tile([P, width], F32, name="tanh_cell")
             for unit, part in zip(units, parts):
                 nc.scalar.activation(tanh_cell[:, part], cells[unit][:], TANH)
@@ -139,4 +172,4 @@ def tile_treelstm_kernel(tc, base, x, w, b, offs, out):
             if all(later[0][0] != h for later in scatters[q + 1 :]):
                 nc.sync.dma_start(out_blocks[h], windows[h][:])
             if q in by_squares:
-                factors[by_squares[q]] = factors_of(*by_squares[q])
+                factors[by_squares[q]] = pairs_of(by_squares[q][1])

@@ -45,6 +45,10 @@ def tile_treelstm_kernel(tc, base, x, w, b, offs, out):
 
         one = held.tile([P, P], F32, name="one")
         make_identity(nc, one[:])
+        swap = held.tile([P, P], F32, name="swap")
+        nc.gpsimd.memset(swap[:], 0.0)
+        nc.gpsimd.tensor_copy(swap[LOW, HIGH], one[LOW, LOW])
+        nc.gpsimd.tensor_copy(swap[HIGH, LOW], one[HIGH, HIGH])
         mix = held.tile([P, P], F32, name="mix")
         nc.gpsimd.tensor_scalar(mix[LOW, LOW], one[LOW, LOW], 0.5, None, MULT)
         nc.gpsimd.tensor_scalar(mix[LOW, HIGH], one[LOW, LOW], 0.5, None, MULT)
@@ -63,21 +67,23 @@ def tile_treelstm_kernel(tc, base, x, w, b, offs, out):
         nc.sync.dma_start(offsets[:], offs)
         windows = [held.tile([P, S], F32, name=f"window{h}") for h in range(BLOCKS)]
         nc.sync.dma_start(windows[0][:], base_blocks[0])
-        bias_pair = held.tile([P, 2], F32, name="bias_pair")
-        b_pair = b.rearrange("(g k c h) o -> g h c (k o)", g=GATES, k=2, h=BLOCKS)
-        with nc.allow_non_contiguous_dma(reason="256 single values, loaded once"):
-            nc.sync.dma_start(bias_pair[LOW, :], b_pair[IN_GATE, 1])
-            nc.sync.dma_start(bias_pair[HIGH, :], b_pair[UPD, 1])
         for start in range(X_LOAD, N, X_LOAD):
             nc.sync.dma_start(x_sb[start][:], x[:, start : start + X_LOAD])
-        nc.scalar.mul(bias_pair[LOW, :], bias_pair[LOW, :], 0.5)
+        for h in range(1, BLOCKS):
+            nc.sync.dma_start(windows[h][:], base_blocks[h])
+
+        swapped = banks.tile([P, BIAS_ROWS], F32, name="swapped", tag="z")
+        nc.tensor.matmul(swapped[:], swap[:], bias[:], start=True, stop=True)
+        bias_pair = held.tile([P, 2], F32, name="bias_pair")
+        of_in, of_upd = IN_GATE * BLOCKS + 1, UPD * BLOCKS + 1
+        for k, (low, high) in enumerate(((bias, swapped), (swapped, bias))):
+            nc.vector.tensor_scalar(bias_pair[LOW, k : k + 1], low[LOW, of_in : of_in + 1], 0.5, None, MULT)
+            nc.vector.tensor_copy(bias_pair[HIGH, k : k + 1], high[HIGH, of_upd : of_upd + 1])
         w_pair = held.tile([DIN, 2 * P], BF16, name="w_pair")
         w_pair_parts = w_pair[:].rearrange("d (k s c) -> s d k c", k=2, s=2)
         for part, g, factor in ((0, IN_GATE, 0.5), (1, UPD, 1.0)):
             columns = w_sb[:, g * H + 1 : (g + 1) * H : BLOCKS].rearrange("d (k c) -> d k c", k=2)
             nc.vector.tensor_scalar(w_pair_parts[part], columns, factor, None, MULT)
-        for h in range(1, BLOCKS):
-            nc.sync.dma_start(windows[h][:], base_blocks[h])
 
         def gate(g, h, first, values, func):
             k = g * BLOCKS + h
@@ -145,7 +151,7 @@ def tile_treelstm_kernel(tc, base, x, w, b, offs, out):
             [(1, PIECE), (1, 2 * PIECE)],
         ]
         by_vector = [(0, 0), (0, PIECE), (1, 3 * PIECE), (0, 2 * PIECE), (0, 3 * PIECE)]
-        by_squares = {0: (1, 0), 2: (1, PIECE), 4: (1, 2 * PIECE)}
+        by_squares = {0: (1, 0), 2: (1, PIECE), 3: (1, 2 * PIECE)}
         factors, sums, cells = {}, {}, {}
 
         cells[by_vector[0]] = product_of(*factors_of(*by_vector[0]))

@@ -85,17 +85,20 @@ def tile_treelstm_kernel(tc, base, x, w, b, offs, out):
             columns = w_sb[:, g * H + 1 : (g + 1) * H : BLOCKS].rearrange("d (k c) -> d k c", k=2)
             nc.vector.tensor_scalar(w_pair_parts[part], columns, factor, None, MULT)
 
-        def gate(g, h, first, values, func):
-            k = g * BLOCKS + h
+        def z_of(weights, first):
             start = first - first % X_LOAD
             z = banks.tile([P, PIECE], F32, name="z")
             nc.tensor.matmul(
-                z[:],
-                w_sb[:, g * H + h : (g + 1) * H : BLOCKS],
-                x_sb[start][:, first - start : first - start + PIECE],
-                start=True,
-                stop=True,
+                z[:], weights, x_sb[start][:, first - start : first - start + PIECE], start=True, stop=True
             )
+            return z
+
+        def gate_z(g, h, first):
+            return z_of(w_sb[:, g * H + h : (g + 1) * H : BLOCKS], first)
+
+        def gate(g, h, first, values, func):
+            k = g * BLOCKS + h
+            z = made_early.get((g, h, first)) or gate_z(g, h, first)
             nc.scalar.activation(values, z[:], func, bias=bias[:, k : k + 1])
 
         def factors_of(h, first):
@@ -110,18 +113,12 @@ def tile_treelstm_kernel(tc, base, x, w, b, offs, out):
             nc.vector.tensor_tensor(cell[:], in_gate[:], upd[:], MULT)
             return cell
 
-        def pairs_of(first):
+        def pair_zs(first):
+            return [z_of(w_pair[:, k * P : (k + 1) * P], first) for k in range(2)]
+
+        def pairs_of(zs):
             pairs = []
-            for k in range(2):
-                z = banks.tile([P, PIECE], F32, name="z")
-                start = first - first % X_LOAD
-                nc.tensor.matmul(
-                    z[:],
-                    w_pair[:, k * P : (k + 1) * P],
-                    x_sb[start][:, first - start : first - start + PIECE],
-                    start=True,
-                    stop=True,
-                )
+            for k, z in enumerate(zs):
                 pair = gates.tile([P, PIECE], F32, name=f"pair{k}")
                 nc.scalar.activation(pair[:], z[:], TANH, bias=bias_pair[:, k : k + 1])
                 pairs.append(pair)
@@ -152,7 +149,7 @@ def tile_treelstm_kernel(tc, base, x, w, b, offs, out):
         ]
         by_vector = [(0, 0), (0, PIECE), (1, 3 * PIECE), (0, 2 * PIECE), (0, 3 * PIECE)]
         by_squares = {0: (1, 0), 2: (1, PIECE), 3: (1, 2 * PIECE)}
-        factors, sums, cells = {}, {}, {}
+        factors, sums, cells, made_early = {}, {}, {}, {}
 
         cells[by_vector[0]] = product_of(*factors_of(*by_vector[0]))
         for q, units in enumerate(scatters):
@@ -178,4 +175,9 @@ def tile_treelstm_kernel(tc, base, x, w, b, offs, out):
             if all(later[0][0] != h for later in scatters[q + 1 :]):
                 nc.sync.dma_start(out_blocks[h], windows[h][:])
             if q in by_squares:
-                factors[by_squares[q]] = pairs_of(by_squares[q][1])
+                first = by_squares[q][1]
+                factors[by_squares[q]] = pairs_of(made_early.get(first) or pair_zs(first))
+            if q == 0:
+                (h, first) = scatters[1][0]
+                made_early[OUT_GATE, h, first] = gate_z(OUT_GATE, h, first)
+                made_early[PIECE] = pair_zs(PIECE)

import concourse.mybir as mybir
from concourse.masks import make_identity

F32 = mybir.dt.float32
BF16 = mybir.dt.bfloat16
U16 = mybir.dt.uint16
SIGMOID = mybir.ActivationFunctionType.Sigmoid
TANH = mybir.ActivationFunctionType.Tanh
SQUARE = mybir.ActivationFunctionType.Square
MULT = mybir.AluOpType.mult

P = 128
HALF = P // 2
LOW, HIGH = slice(0, HALF), slice(HALF, P)
DIN, H, GATES, S, N = 128, 256, 3, 4096, 2048
BLOCKS = H // P
BANK = 512
PIECE = BANK
X_LOAD = 1024
PER_COLUMN = 16
IN_GATE, OUT_GATE, UPD = 0, 1, 2
BIAS_ROWS = GATES * BLOCKS

FLOPS = 2 * DIN * GATES * H * N


def tile_treelstm_kernel(tc, base, x, w, b, offs, out):
    nc = tc.nc
    with (
        tc.tile_pool(name="held", bufs=1) as held,
        tc.tile_pool(name="gates", bufs=BLOCKS * (N // PIECE) - 1) as gates,
        tc.psum_pool(name="banks", bufs=8) as banks,
    ):
        bias = held.tile([P, BIAS_ROWS], F32, name="bias")
        with nc.allow_non_contiguous_dma(reason="384 runs of two values, loaded once"):
            nc.scalar.dma_start(
                bias[:].rearrange("p (g h) -> p g h", g=GATES),
                b.rearrange("(g p h) o -> p g (h o)", g=GATES, h=BLOCKS),
            )
        base_blocks = base.rearrange("(p h) s -> h p s", h=BLOCKS)
        out_blocks = out.rearrange("(p h) s -> h p s", h=BLOCKS)
        scratch = held.tile([P, 1], F32, name="scratch")
        nc.gpsimd.memset(scratch[:], 0.0)
        nc.scalar.activation(scratch[:], scratch[:], SIGMOID)

        one = held.tile([P, P], F32, name="one")
        make_identity(nc, one[:])
        swap = held.tile([P, P], F32, name="swap")
        nc.gpsimd.memset(swap[:], 0.0)
        nc.gpsimd.tensor_copy(swap[LOW, HIGH], one[LOW, LOW])
        nc.gpsimd.tensor_copy(swap[HIGH, LOW], one[HIGH, HIGH])
        mix = held.tile([P, P], F32, name="mix")
        nc.gpsimd.tensor_scalar(mix[LOW, LOW], one[LOW, LOW], 0.5, None, MULT)
        nc.gpsimd.tensor_scalar(mix[LOW, HIGH], one[LOW, LOW], 0.5, None, MULT)
        nc.gpsimd.tensor_copy(mix[HIGH, LOW], one[HIGH, HIGH])
        nc.gpsimd.tensor_scalar(mix[HIGH, HIGH], one[HIGH, HIGH], -1.0, None, MULT)
        spread = held.tile([P, 3 * HALF], F32, name="spread")
        nc.gpsimd.memset(spread[:], 0.0)
        nc.gpsimd.tensor_copy(spread[LOW, HIGH], one[LOW, LOW])
        nc.gpsimd.tensor_scalar(spread[HIGH, HIGH], one[HIGH, HIGH], -1.0, None, MULT)

        w_sb = held.tile([DIN, GATES * H], BF16, name="w_sb")
        nc.sync.dma_start(w_sb[:], w)
        x_sb = {start: held.tile([DIN, X_LOAD], BF16, name=f"x_sb{start}") for start in range(0, N, X_LOAD)}
        nc.sync.dma_start(x_sb[0][:], x[:, 0:X_LOAD])
        offsets = held.tile([P, N // PER_COLUMN], U16, name="offsets")
        nc.sync.dma_start(offsets[:], offs)
        windows = [held.tile([P, S], F32, name=f"window{h}") for h in range(BLOCKS)]
        nc.sync.dma_start(windows[0][:], base_blocks[0])
        for start in range(X_LOAD, N, X_LOAD):
            nc.sync.dma_start(x_sb[start][:], x[:, start : start + X_LOAD])
        for h in range(1, BLOCKS):
            nc.sync.dma_start(windows[h][:], base_blocks[h])

        swapped = banks.tile([P, BIAS_ROWS], F32, name="swapped", tag="z")
        nc.tensor.matmul(swapped[:], swap[:], bias[:], start=True, stop=True)
        bias_pair = held.tile([P, 2], F32, name="bias_pair")
        of_in, of_upd = IN_GATE * BLOCKS + 1, UPD * BLOCKS + 1
        for k, (low, high) in enumerate(((bias, swapped), (swapped, bias))):
            nc.vector.tensor_scalar(bias_pair[LOW, k : k + 1], low[LOW, of_in : of_in + 1], 0.5, None, MULT)
            nc.vector.tensor_copy(bias_pair[HIGH, k : k + 1], high[HIGH, of_upd : of_upd + 1])
        w_pair = held.tile([DIN, 2 * P], BF16, name="w_pair")
        w_pair_parts = w_pair[:].rearrange("d (k s c) -> s d k c", k=2, s=2)
        for part, g, factor in ((0, IN_GATE, 0.5), (1, UPD, 1.0)):
            columns = w_sb[:, g * H + 1 : (g + 1) * H : BLOCKS].rearrange("d (k c) -> d k c", k=2)
            nc.vector.tensor_scalar(w_pair_parts[part], columns, factor, None, MULT)

        def z_of(weights, first):
            start = first - first % X_LOAD
            z = banks.tile([P, PIECE], F32, name="z")
            nc.tensor.matmul(
                z[:], weights, x_sb[start][:, first - start : first - start + PIECE], start=True, stop=True
            )
            return z

        def gate_z(g, h, first):
            return z_of(w_sb[:, g * H + h : (g + 1) * H : BLOCKS], first)

        def gate(g, h, first, values, func):
            k = g * BLOCKS + h
            z = made_early.get((g, h, first)) or gate_z(g, h, first)
            nc.scalar.activation(values, z[:], func, bias=bias[:, k : k + 1])

        def factors_of(h, first):
            in_gate = gates.tile([P, PIECE], F32, name="in_gate")
            gate(IN_GATE, h, first, in_gate[:], SIGMOID)
            upd = gates.tile([P, PIECE], F32, name="upd")
            gate(UPD, h, first, upd[:], TANH)
            return in_gate, upd

        def product_of(in_gate, upd):
            cell = gates.tile([P, PIECE], F32, name="cell")
            nc.vector.tensor_tensor(cell[:], in_gate[:], upd[:], MULT)
            return cell

        def pair_zs(first):
            return [z_of(w_pair[:, k * P : (k + 1) * P], first) for k in range(2)]

        def pairs_of(zs):
            pairs = []
            for k, z in enumerate(zs):
                pair = gates.tile([P, PIECE], F32, name=f"pair{k}")
                nc.scalar.activation(pair[:], z[:], TANH, bias=bias_pair[:, k : k + 1])
                pairs.append(pair)
            return pairs

        def mixed(pair):
            z = banks.tile([P, PIECE], F32, name="z")
            nc.tensor.matmul(z[:], mix[:], pair[:], start=True, stop=True)
            return z

        def product_by_squares(sums):
            cell = banks.tile([P, PIECE], F32, name="z")
            for k, z in enumerate(sums):
                square = gates.tile([P, PIECE], F32, name=f"square{k}")
                nc.scalar.activation(square[:], z[:], SQUARE, bias=0.25, scale=0.5)
                place = spread[:, (1 - k) * HALF : (1 - k) * HALF + P]
                nc.tensor.matmul(cell[:], place, square[:], start=k == 0, stop=k == 1)
            return cell

        scatters = [
            [(0, 0)],
            [(0, PIECE)],
            [(1, 3 * PIECE)],
            [(0, 2 * PIECE)],
            [(1, 0)],
            [(0, 3 * PIECE)],
            [(1, PIECE), (1, 2 * PIECE)],
        ]
        by_vector = [(0, 0), (0, PIECE), (1, 3 * PIECE), (0, 2 * PIECE), (0, 3 * PIECE)]
        by_squares = {0: (1, 0), 2: (1, PIECE), 3: (1, 2 * PIECE)}
        factors, sums, cells, made_early = {}, {}, {}, {}

        cells[by_vector[0]] = product_of(*factors_of(*by_vector[0]))
        for q, units in enumerate(scatters):
            if q + 1 < len(by_vector):
                cells[by_vector[q + 1]] = product_of(*factors_of(*by_vector[q + 1]))
            h, first = units[0]
            width = len(units) * PIECE
            parts = [slice(at, at + PIECE) for at in range(0, width, PIECE)]
            out_gate = gates.tile([P, width], F32, name="out_gate")
            for unit, part in zip(units, parts):
                gate(OUT_GATE, *unit, out_gate[:, part], SIGMOID)
            for begin, unit in by_squares.items():
                if q == begin + 1:
                    sums[unit] = [mixed(pair) for pair in factors[unit]]
                elif q == begin + 2:
                    cells[unit] = product_by_squares(sums[unit])
            tanh_cell = gates.tile([P, width], F32, name="tanh_cell")
            for unit, part in zip(units, parts):
                nc.scalar.activation(tanh_cell[:, part], cells[unit][:], TANH)

            listed = offsets[:, first // PER_COLUMN : (first + width) // PER_COLUMN]
            nc.vector.tensor_tensor(windows[h][:].indirect(listed), out_gate[:], tanh_cell[:], MULT)
            if all(later[0][0] != h for later in scatters[q + 1 :]):
                nc.sync.dma_start(out_blocks[h], windows[h][:])
            if q in by_squares:
                first = by_squares[q][1]
                factors[by_squares[q]] = pairs_of(made_early.get(first) or pair_zs(first))
            if q == 0:
                (h, first) = scatters[1][0]
                made_early[OUT_GATE, h, first] = gate_z(OUT_GATE, h, first)
                made_early[PIECE] = pair_zs(PIECE)
